import numpy as np
import ml_dtypes


def mxq(x, axis, fmt="e4m3"):
    dtype, down = {"e4m3": (ml_dtypes.float8_e4m3fn, 7), "e5m2": (ml_dtypes.float8_e5m2, 14)}[fmt]
    v = np.moveaxis(np.asarray(x, np.float32).astype(ml_dtypes.bfloat16).astype(np.float64), axis, -1)
    blocks = v.reshape(v.shape[:-1] + (-1, 32))
    amax = np.abs(blocks).max(-1, keepdims=True)
    byte = np.maximum(np.where(amax > 0, np.frexp(amax)[1] - 1 + 127, 0) - down, 1)
    scale = np.exp2(byte - 127.0)
    codes = (blocks / scale).astype(np.float32).astype(dtype).astype(np.float64)
    return np.moveaxis((codes * scale).reshape(v.shape), -1, axis)


WIDE = False


def mx_kscale(k):
    if not WIDE:
        return np.ones(k)
    levels = np.array([10, -10, 5, -5, 0])
    if k % 512:
        return np.exp2(np.random.permutation(np.resize(levels, k // 32))).repeat(32)
    a = np.empty((k // 512, 16))
    for p in range(k // 512):
        a[p, :8] = np.random.permutation(np.resize(levels, 8))
        for g in range(8):
            far = levels[np.abs(levels - a[p, g]) >= 10]
            a[p, g + 8] = far[np.random.randint(len(far))]
    return np.exp2(a.ravel()).repeat(32)


BF16 = ml_dtypes.bfloat16


def bf(x):
    return np.asarray(x, np.float32).astype(BF16)


def f64(x):
    return np.asarray(x).astype(np.float64)


B, S, H, D, M = 2, 64, 16, 64, 1024
E = H * D
R = B * S
EPS = 1e-6


def setup_inputs():
    s = mx_kscale(E)
    return {"query_input": bf(np.random.standard_normal((B, S, E))),
            "norm_query_w": bf((1.0 + 0.1 * np.random.standard_normal(E)) * s),
            "W_in": bf(np.random.standard_normal((E, E)) / np.sqrt(E) / s[None, :])}


def reference(query_input, norm_query_w, W_in):
    x = f64(query_input).reshape(R, E)
    normed = x * (1.0 / np.sqrt(np.mean(x * x, 1, keepdims=True) + EPS))
    h = normed * f64(norm_query_w)
    return (mxq(h, 1, "e4m3") @ mxq(f64(W_in), 1, "e4m3").T).reshape(B, S, E)

@@ -1,0 +1,226 @@
+from contextlib import ExitStack
+
+import concourse.mybir as mybir
+from concourse.masks import make_identity
+
+F32 = mybir.dt.float32
+BF16 = mybir.dt.bfloat16
+U32 = mybir.dt.uint32
+U8 = mybir.dt.uint8
+FP8X4 = mybir.dt.float8_e4m3fn_x4
+ACT = mybir.ActivationFunctionType
+ALU = mybir.AluOpType
+
+P = 128
+E = 1024
+EPS = 1e-6
+PACK = 4
+PASSES = E // (P * PACK)
+WORDS = 2 * PASSES
+CHUNKS = E // P
+HEAD_CHUNKS = 2
+PAIR = 2 * P
+HALF = E // 2
+HEAD_WARM_UP = 16
+STREAM_WARM_UP = 6
+
+FLOPS = 2 * P * E * E
+
+
+def word_cols(j):
+    s, u = divmod(j, 2)
+    return slice(2 * P * s + u, 2 * P * (s + 1), 2)
+
+
+def tile_hopfieldmemorylayer_pa_s_kernel(tc, query_input, norm_query_w, W_in, out):
+    nc = tc.nc
+    x_dram = query_input.flatten_outer_dims()
+    out_dram = out.flatten_outer_dims()
+
+    with ExitStack() as ctx:
+        keep = ctx.enter_context(tc.tile_pool(name="keep", bufs=1))
+        w_pool = ctx.enter_context(tc.tile_pool(name="w_rows", bufs=CHUNKS))
+        grouped_pool = ctx.enter_context(tc.tile_pool(name="grouped", bufs=CHUNKS))
+        psum_w = ctx.enter_context(tc.psum_pool(name="psum_w", bufs=4))
+        psum_misc = ctx.enter_context(tc.psum_pool(name="psum_misc", bufs=4))
+        ctx.enter_context(tc.manual_schedule())
+
+        x_sb = keep.tile([P, E], BF16)
+        nc.sync.dma_start(out=x_sb[:], in_=x_dram)
+        g_rows = keep.tile([P, PACK * P], BF16)
+        nc.vector.memset(g_rows[:], 0.0)
+        nc.sync.dma_start(
+            out=g_rows[0:PASSES, :], in_=norm_query_w.rearrange("(j c) -> j c", j=PASSES)
+        )
+
+        w_rows = []
+        for c in range(CHUNKS):
+            rows = w_pool.tile([P, E], BF16, name="rows", tag="rows")
+            nc.sync.dma_start(out=rows[:], in_=W_in[c * P : (c + 1) * P, :])
+            w_rows.append(rows)
+
+        identity = keep.tile([P, P], F32)
+        make_identity(nc, identity[:])
+
+        eps = keep.tile([P, 1], F32)
+        nc.vector.memset(eps[:], EPS)
+        table_warmer = keep.tile([P, 1], F32)
+        nc.scalar.activation(out=table_warmer[:], in_=eps[:], func=ACT.Sqrt)
+
+        idle_values = keep.tile([P, PACK * P], BF16, align_bytes=64)
+        nc.vector.memset(idle_values[:], 0.0)
+        idle_codes = keep.tile([P, P], U32, align_bytes=64)
+        idle_scales = keep.tile([P, P], U8, align_bytes=64)
+        nc.vector.quantize_mx(
+            out=idle_codes[:].bitcast(FP8X4), scales=idle_scales[:], in_=idle_values[:]
+        )
+        idle_bank = psum_misc.tile([P, P], F32, tag="bank")
+        for i in range(HEAD_WARM_UP):
+            nc.tensor.matmul_mx(
+                out=idle_bank[:],
+                lhsT=idle_codes[:].bitcast(FP8X4),
+                lhsT_scale=idle_scales[:],
+                rhs=idle_codes[:].bitcast(FP8X4),
+                rhs_scale=idle_scales[:],
+                start=True,
+                stop=True,
+            )
+
+        x_t = psum_misc.tile([P, WORDS, P], F32, tag="bank")
+        x_words = x_sb[:].bitcast(F32)
+        for j in range(WORDS):
+            nc.tensor.transpose(x_t[:, j, :], x_words[:, word_cols(j)], identity[:])
+
+        g_t = psum_misc.tile([P, 2, P], F32, tag="bank")
+        g_words = g_rows[:].bitcast(F32)
+        for u in range(2):
+            nc.tensor.transpose(g_t[:, u, :], g_words[:, u : 2 * P : 2], identity[:])
+
+        squares_a = keep.tile([P, HALF], F32)
+        sum_a = keep.tile([P, 1], F32)
+        nc.scalar.activation(
+            out=squares_a[:], in_=x_sb[:, 0:HALF], func=ACT.Square, accum_out=sum_a[:]
+        )
+        squares_b = keep.tile([P, HALF], F32)
+        sum_b = keep.tile([P, 1], F32)
+        nc.vector.scalar_tensor_tensor(
+            out=squares_b[:],
+            in0=x_sb[:, HALF:E],
+            scalar=1.0,
+            in1=x_sb[:, HALF:E],
+            op0=ALU.mult,
+            op1=ALU.mult,
+            accum_out=sum_b[:],
+        )
+        mean_b_eps = keep.tile([P, 1], F32)
+        nc.vector.tensor_scalar(
+            out=mean_b_eps[:], in0=sum_b[:], scalar1=1.0 / E, scalar2=EPS, op0=ALU.mult, op1=ALU.add
+        )
+        rms = keep.tile([P, 1], F32)
+        nc.scalar.activation(
+            out=rms[:], in_=sum_a[:], func=ACT.Sqrt, scale=1.0 / E, bias=mean_b_eps[:]
+        )
+        inv_rms = keep.tile([P, 1], F32)
+
+        g_pairs = keep.tile([P, WORDS], F32)
+        nc.vector.tensor_copy(
+            out=g_pairs[:].rearrange("p (s u) -> p s u", u=2),
+            in_=g_t[:, :, 0:PASSES].rearrange("p u s -> p s u"),
+        )
+        g_values = g_pairs[:].bitcast(BF16)
+        xg = keep.tile([P, PASSES, P, PACK], F32)
+
+        def gain(s):
+            nc.vector.tensor_tensor(
+                out=xg[:, s, :, :].rearrange("p r (u e) -> p r u e", e=2),
+                in0=x_t[:, 2 * s : 2 * s + 2, :]
+                .bitcast(BF16)
+                .rearrange("p u (r e) -> p r u e", e=2),
+                in1=g_values[:, PACK * s : PACK * (s + 1)]
+                .rearrange("p (u e) -> p u e", e=2)
+                .unsqueeze(1)
+                .to_broadcast([P, P, 2, 2]),
+                op=ALU.mult,
+            )
+
+        gain(0)
+        nc.vector.reciprocal(out=inv_rms[:], in_=rms[:])
+        gain(1)
+
+        w_codes = keep.tile([P, CHUNKS, PASSES * P], U32, align_bytes=64)
+        w_scales = keep.tile([P, CHUNKS, PASSES * P], U8, align_bytes=64)
+        w_grouped = {}
+
+        def transpose_chunk(c):
+            w_t = psum_w.tile([P, WORDS, P], F32, name="w_t", tag="w_t")
+            words = w_rows[c][:].bitcast(F32)
+            for j in range(WORDS):
+                nc.tensor.transpose(w_t[:, j, :], words[:, word_cols(j)], identity[:])
+            if c < STREAM_WARM_UP:
+                nc.tensor.matmul(
+                    out=idle_bank[:], lhsT=identity[:], rhs=identity[:], start=True, stop=True
+                )
+            grouped = grouped_pool.tile(
+                [P, PASSES, P, PACK], BF16, name="grouped", tag="grouped", align_bytes=64
+            )
+            nc.scalar.copy(
+                out=grouped[:].bitcast(F32),
+                in_=w_t[:].rearrange("p (s u) o -> p s o u", u=2),
+            )
+            w_grouped[c] = grouped
+
+        def quantise_chunk(c):
+            nc.vector.quantize_mx(
+                out=w_codes[:, c, :].bitcast(FP8X4),
+                scales=w_scales[:, c, :],
+                in_=w_grouped[c][:].rearrange("p s o t -> p (s o t)"),
+            )
+
+        for c in range(HEAD_CHUNKS):
+            transpose_chunk(c)
+
+        inv_rms_t = psum_misc.tile([P, P], F32, tag="bank")
+        nc.tensor.transpose(inv_rms_t[:], inv_rms[:, 0:1].to_broadcast([P, P]), identity[:])
+        h_grouped = keep.tile([P, PASSES, P, PACK], BF16, align_bytes=64)
+        nc.vector.tensor_tensor(
+            out=h_grouped[:],
+            in0=xg[:],
+            in1=inv_rms_t[:].unsqueeze(1).unsqueeze(3).to_broadcast([P, PASSES, P, PACK]),
+            op=ALU.mult,
+        )
+        h_codes = keep.tile([P, PASSES * P], U32, align_bytes=64)
+        h_scales = keep.tile([P, PASSES * P], U8, align_bytes=64)
+        nc.vector.quantize_mx(
+            out=h_codes[:].bitcast(FP8X4),
+            scales=h_scales[:],
+            in_=h_grouped[:].rearrange("p s r t -> p (s r t)"),
+        )
+
+        for c in range(HEAD_CHUNKS):
+            quantise_chunk(c)
+        for c in range(HEAD_CHUNKS, CHUNKS):
+            transpose_chunk(c)
+            quantise_chunk(c)
+
+        out_sb = keep.tile([P, E], F32)
+        for pair in range(E // PAIR):
+            acc = psum_misc.tile([P, PAIR], F32, tag="bank")
+            for half in range(2):
+                c = 2 * pair + half
+                for s in range(PASSES):
+                    k_cols = slice(s * P, (s + 1) * P)
+                    nc.tensor.matmul_mx(
+                        out=acc[:, half * P : (half + 1) * P],
+                        lhsT=h_codes[:, k_cols].bitcast(FP8X4),
+                        lhsT_scale=h_scales[:, k_cols],
+                        rhs=w_codes[:, c, k_cols].bitcast(FP8X4),
+                        rhs_scale=w_scales[:, c, k_cols],
+                        start=(s == 0),
+                        stop=(s == PASSES - 1),
+                    )
+            cols = slice(pair * PAIR, (pair + 1) * PAIR)
+            if pair == E // PAIR - 1:
+                nc.vector.tensor_copy(out=out_sb[:, cols], in_=acc[:])
+            else:
+                nc.scalar.copy(out=out_sb[:, cols], in_=acc[:])
+            nc.sync.dma_start(out=out_dram[:, cols], in_=out_sb[:, cols])

@@ -15,14 +15,13 @@ P = 128
 E = 1024
 EPS = 1e-6
 PACK = 4
-PASSES = E // (P * PACK)
+K_PASS = P * PACK
+PASSES = E // K_PASS
 WORDS = 2 * PASSES
 CHUNKS = E // P
-HEAD_CHUNKS = 2
 PAIR = 2 * P
-HALF = E // 2
-HEAD_WARM_UP = 16
-STREAM_WARM_UP = 6
+SCALAR_SQUARES = 640
+HEAD_WARM_UP = 8
 
 FLOPS = 2 * P * E * E
 
@@ -45,14 +44,10 @@ def tile_hopfieldmemorylayer_pa_s_kernel(tc, query_input, norm_query_w, W_in, ou
         psum_misc = ctx.enter_context(tc.psum_pool(name="psum_misc", bufs=4))
         ctx.enter_context(tc.manual_schedule())
 
+        g_sb = keep.tile([P, E // P], BF16)
+        nc.scalar.dma_start(out=g_sb[:], in_=norm_query_w.rearrange("(p c) -> p c", p=P))
         x_sb = keep.tile([P, E], BF16)
         nc.sync.dma_start(out=x_sb[:], in_=x_dram)
-        g_rows = keep.tile([P, PACK * P], BF16)
-        nc.vector.memset(g_rows[:], 0.0)
-        nc.sync.dma_start(
-            out=g_rows[0:PASSES, :], in_=norm_query_w.rearrange("(j c) -> j c", j=PASSES)
-        )
-
         w_rows = []
         for c in range(CHUNKS):
             rows = w_pool.tile([P, E], BF16, name="rows", tag="rows")
@@ -62,12 +57,12 @@ def tile_hopfieldmemorylayer_pa_s_kernel(tc, query_input, norm_query_w, W_in, ou
         identity = keep.tile([P, P], F32)
         make_identity(nc, identity[:])
 
-        eps = keep.tile([P, 1], F32)
-        nc.vector.memset(eps[:], EPS)
+        one = keep.tile([P, 1], F32)
+        nc.vector.memset(one[:], 1.0)
         table_warmer = keep.tile([P, 1], F32)
-        nc.scalar.activation(out=table_warmer[:], in_=eps[:], func=ACT.Sqrt)
+        nc.scalar.activation(out=table_warmer[:], in_=one[:], func=ACT.Abs_reciprocal_sqrt)
 
-        idle_values = keep.tile([P, PACK * P], BF16, align_bytes=64)
+        idle_values = keep.tile([P, K_PASS], BF16, align_bytes=64)
         nc.vector.memset(idle_values[:], 0.0)
         idle_codes = keep.tile([P, P], U32, align_bytes=64)
         idle_scales = keep.tile([P, P], U8, align_bytes=64)
@@ -86,28 +81,25 @@ def tile_hopfieldmemorylayer_pa_s_kernel(tc, query_input, norm_query_w, W_in, ou
                 stop=True,
             )
 
-        x_t = psum_misc.tile([P, WORDS, P], F32, tag="bank")
-        x_words = x_sb[:].bitcast(F32)
-        for j in range(WORDS):
-            nc.tensor.transpose(x_t[:, j, :], x_words[:, word_cols(j)], identity[:])
+        g_all = psum_misc.tile([P, P, WORDS], F32, tag="bank")
+        g_words = g_sb[:].bitcast(F32)
+        for i in range(WORDS):
+            nc.tensor.transpose(
+                g_all[:, :, i], g_words[:, i : i + 1].to_broadcast([P, P]), identity[:]
+            )
 
-        g_t = psum_misc.tile([P, 2, P], F32, tag="bank")
-        g_words = g_rows[:].bitcast(F32)
-        for u in range(2):
-            nc.tensor.transpose(g_t[:, u, :], g_words[:, u : 2 * P : 2], identity[:])
-
-        squares_a = keep.tile([P, HALF], F32)
+        squares_a = keep.tile([P, SCALAR_SQUARES], F32)
         sum_a = keep.tile([P, 1], F32)
         nc.scalar.activation(
-            out=squares_a[:], in_=x_sb[:, 0:HALF], func=ACT.Square, accum_out=sum_a[:]
+            out=squares_a[:], in_=x_sb[:, 0:SCALAR_SQUARES], func=ACT.Square, accum_out=sum_a[:]
         )
-        squares_b = keep.tile([P, HALF], F32)
+        squares_b = keep.tile([P, E - SCALAR_SQUARES], F32)
         sum_b = keep.tile([P, 1], F32)
         nc.vector.scalar_tensor_tensor(
             out=squares_b[:],
-            in0=x_sb[:, HALF:E],
+            in0=x_sb[:, SCALAR_SQUARES:E],
             scalar=1.0,
-            in1=x_sb[:, HALF:E],
+            in1=x_sb[:, SCALAR_SQUARES:E],
             op0=ALU.mult,
             op1=ALU.mult,
             accum_out=sum_b[:],
@@ -116,58 +108,62 @@ def tile_hopfieldmemorylayer_pa_s_kernel(tc, query_input, norm_query_w, W_in, ou
         nc.vector.tensor_scalar(
             out=mean_b_eps[:], in0=sum_b[:], scalar1=1.0 / E, scalar2=EPS, op0=ALU.mult, op1=ALU.add
         )
-        rms = keep.tile([P, 1], F32)
-        nc.scalar.activation(
-            out=rms[:], in_=sum_a[:], func=ACT.Sqrt, scale=1.0 / E, bias=mean_b_eps[:]
-        )
         inv_rms = keep.tile([P, 1], F32)
-
-        g_pairs = keep.tile([P, WORDS], F32)
-        nc.vector.tensor_copy(
-            out=g_pairs[:].rearrange("p (s u) -> p s u", u=2),
-            in_=g_t[:, :, 0:PASSES].rearrange("p u s -> p s u"),
+        nc.scalar.activation(
+            out=inv_rms[:],
+            in_=sum_a[:],
+            func=ACT.Abs_reciprocal_sqrt,
+            scale=1.0 / E,
+            bias=mean_b_eps[:],
         )
-        g_values = g_pairs[:].bitcast(BF16)
-        xg = keep.tile([P, PASSES, P, PACK], F32)
 
-        def gain(s):
-            nc.vector.tensor_tensor(
-                out=xg[:, s, :, :].rearrange("p r (u e) -> p r u e", e=2),
-                in0=x_t[:, 2 * s : 2 * s + 2, :]
-                .bitcast(BF16)
-                .rearrange("p u (r e) -> p r u e", e=2),
-                in1=g_values[:, PACK * s : PACK * (s + 1)]
-                .rearrange("p (u e) -> p u e", e=2)
-                .unsqueeze(1)
-                .to_broadcast([P, P, 2, 2]),
-                op=ALU.mult,
+        h_rows = keep.tile([P, E], BF16)
+        g_bf16 = g_all[:].rearrange("r p i -> r (p i)").bitcast(BF16)
+
+        def normalise(s):
+            cols = slice(s * K_PASS, (s + 1) * K_PASS)
+            nc.vector.scalar_tensor_tensor(
+                out=h_rows[:, cols],
+                in0=x_sb[:, cols],
+                scalar=inv_rms[:],
+                in1=g_bf16[:, cols],
+                op0=ALU.mult,
+                op1=ALU.mult,
             )
 
-        gain(0)
-        nc.vector.reciprocal(out=inv_rms[:], in_=rms[:])
-        gain(1)
+        for s in range(PASSES):
+            normalise(s)
 
         w_codes = keep.tile([P, CHUNKS, PASSES * P], U32, align_bytes=64)
         w_scales = keep.tile([P, CHUNKS, PASSES * P], U8, align_bytes=64)
+        w_turned = {}
         w_grouped = {}
 
-        def transpose_chunk(c):
+        def transpose_chunk(c, passes=range(PASSES)):
             w_t = psum_w.tile([P, WORDS, P], F32, name="w_t", tag="w_t")
             words = w_rows[c][:].bitcast(F32)
-            for j in range(WORDS):
-                nc.tensor.transpose(w_t[:, j, :], words[:, word_cols(j)], identity[:])
-            if c < STREAM_WARM_UP:
-                nc.tensor.matmul(
-                    out=idle_bank[:], lhsT=identity[:], rhs=identity[:], start=True, stop=True
-                )
-            grouped = grouped_pool.tile(
+            for s in passes:
+                for j in (2 * s, 2 * s + 1):
+                    nc.tensor.transpose(w_t[:, j, :], words[:, word_cols(j)], identity[:])
+                w_turned[c, s] = w_t
+
+        def new_group(c):
+            w_grouped[c] = grouped_pool.tile(
                 [P, PASSES, P, PACK], BF16, name="grouped", tag="grouped", align_bytes=64
             )
-            nc.scalar.copy(
-                out=grouped[:].bitcast(F32),
-                in_=w_t[:].rearrange("p (s u) o -> p s o u", u=2),
+
+        def regroup_chunk(c, copy):
+            new_group(c)
+            copy(
+                out=w_grouped[c][:].bitcast(F32),
+                in_=w_turned[c, 0][:].rearrange("p (s u) o -> p s o u", u=2),
             )
-            w_grouped[c] = grouped
+
+        def regroup_pass(c, s, copy):
+            copy(
+                out=w_grouped[c][:, s, :, :].bitcast(F32),
+                in_=w_turned[c, s][:, 2 * s : 2 * s + 2, :].rearrange("p u o -> p o u"),
+            )
 
         def quantise_chunk(c):
             nc.vector.quantize_mx(
@@ -176,31 +172,62 @@ def tile_hopfieldmemorylayer_pa_s_kernel(tc, query_input, norm_query_w, W_in, ou
                 in_=w_grouped[c][:].rearrange("p s o t -> p (s o t)"),
             )
 
-        for c in range(HEAD_CHUNKS):
-            transpose_chunk(c)
+        def quantise_pass(c, s):
+            cols = slice(s * P, (s + 1) * P)
+            nc.vector.quantize_mx(
+                out=w_codes[:, c, cols].bitcast(FP8X4),
+                scales=w_scales[:, c, cols],
+                in_=w_grouped[c][:, s, :, :].rearrange("p o t -> p (o t)"),
+            )
 
-        inv_rms_t = psum_misc.tile([P, P], F32, tag="bank")
-        nc.tensor.transpose(inv_rms_t[:], inv_rms[:, 0:1].to_broadcast([P, P]), identity[:])
+        by_scalar = nc.scalar.copy
+        by_vector = nc.vector.tensor_copy
+
+        transpose_chunk(0)
+        regroup_chunk(0, by_scalar)
+        quantise_chunk(0)
+        transpose_chunk(1)
+        regroup_chunk(1, by_scalar)
+        quantise_chunk(1)
+        transpose_chunk(2)
+        regroup_chunk(2, by_scalar)
+
+        h_t = psum_misc.tile([P, WORDS, P], F32, tag="bank")
+        h_words = h_rows[:].bitcast(F32)
+        for j in range(WORDS):
+            nc.tensor.transpose(h_t[:, j, :], h_words[:, word_cols(j)], identity[:])
         h_grouped = keep.tile([P, PASSES, P, PACK], BF16, align_bytes=64)
-        nc.vector.tensor_tensor(
-            out=h_grouped[:],
-            in0=xg[:],
-            in1=inv_rms_t[:].unsqueeze(1).unsqueeze(3).to_broadcast([P, PASSES, P, PACK]),
-            op=ALU.mult,
+        nc.scalar.copy(
+            out=h_grouped[:].bitcast(F32), in_=h_t[:].rearrange("p (s u) r -> p s r u", u=2)
         )
         h_codes = keep.tile([P, PASSES * P], U32, align_bytes=64)
         h_scales = keep.tile([P, PASSES * P], U8, align_bytes=64)
+
+        quantise_chunk(2)
+        transpose_chunk(3)
+        regroup_chunk(3, by_vector)
         nc.vector.quantize_mx(
             out=h_codes[:].bitcast(FP8X4),
             scales=h_scales[:],
             in_=h_grouped[:].rearrange("p s r t -> p (s r t)"),
         )
-
-        for c in range(HEAD_CHUNKS):
-            quantise_chunk(c)
-        for c in range(HEAD_CHUNKS, CHUNKS):
-            transpose_chunk(c)
-            quantise_chunk(c)
+        transpose_chunk(4)
+        regroup_chunk(4, by_scalar)
+        quantise_chunk(3)
+        quantise_chunk(4)
+        transpose_chunk(5)
+        regroup_chunk(5, by_scalar)
+        quantise_chunk(5)
+        transpose_chunk(6)
+        regroup_chunk(6, by_scalar)
+        for s in range(PASSES):
+            transpose_chunk(7, (s,))
+        new_group(7)
+        regroup_pass(7, 0, by_vector)
+        regroup_pass(7, 1, by_scalar)
+        quantise_chunk(6)
+        quantise_pass(7, 0)
+        quantise_pass(7, 1)
 
         out_sb = keep.tile([P, E], F32)
         for pair in range(E // PAIR):

@@ -21,7 +21,8 @@ WORDS = 2 * PASSES
 CHUNKS = E // P
 PAIR = 2 * P
 SCALAR_SQUARES = 640
-HEAD_WARM_UP = 8
+HEAD_WARM_UP = 14
+STREAM_WARM_UP = 6
 
 FLOPS = 2 * P * E * E
 
@@ -58,12 +59,12 @@ def tile_hopfieldmemorylayer_pa_s_kernel(tc, query_input, norm_query_w, W_in, ou
         make_identity(nc, identity[:])
 
         one = keep.tile([P, 1], F32)
-        nc.vector.memset(one[:], 1.0)
+        nc.gpsimd.memset(one[:], 1.0)
         table_warmer = keep.tile([P, 1], F32)
         nc.scalar.activation(out=table_warmer[:], in_=one[:], func=ACT.Abs_reciprocal_sqrt)
 
         idle_values = keep.tile([P, K_PASS], BF16, align_bytes=64)
-        nc.vector.memset(idle_values[:], 0.0)
+        nc.vector.memset(idle_values[:].bitcast(F32), 0.0)
         idle_codes = keep.tile([P, P], U32, align_bytes=64)
         idle_scales = keep.tile([P, P], U8, align_bytes=64)
         nc.vector.quantize_mx(
@@ -146,6 +147,10 @@ def tile_hopfieldmemorylayer_pa_s_kernel(tc, query_input, norm_query_w, W_in, ou
                 for j in (2 * s, 2 * s + 1):
                     nc.tensor.transpose(w_t[:, j, :], words[:, word_cols(j)], identity[:])
                 w_turned[c, s] = w_t
+            if c < STREAM_WARM_UP:
+                nc.tensor.matmul(
+                    out=idle_bank[:], lhsT=identity[:], rhs=identity[:], start=True, stop=True
+                )
 
         def new_group(c):
             w_grouped[c] = grouped_pool.tile(

@@ -21,8 +21,9 @@ WORDS = 2 * PASSES
 CHUNKS = E // P
 PAIR = 2 * P
 SCALAR_SQUARES = 640
-HEAD_WARM_UP = 14
-STREAM_WARM_UP = 6
+LAST = CHUNKS - 1
+FIRST_SORTED = 3
+HEAD_WARM_UP = 10
 
 FLOPS = 2 * P * E * E
 
@@ -40,6 +41,7 @@ def tile_hopfieldmemorylayer_pa_s_kernel(tc, query_input, norm_query_w, W_in, ou
     with ExitStack() as ctx:
         keep = ctx.enter_context(tc.tile_pool(name="keep", bufs=1))
         w_pool = ctx.enter_context(tc.tile_pool(name="w_rows", bufs=CHUNKS))
+        sorted_pool = ctx.enter_context(tc.tile_pool(name="w_sorted", bufs=CHUNKS - FIRST_SORTED))
         grouped_pool = ctx.enter_context(tc.tile_pool(name="grouped", bufs=CHUNKS))
         psum_w = ctx.enter_context(tc.psum_pool(name="psum_w", bufs=4))
         psum_misc = ctx.enter_context(tc.psum_pool(name="psum_misc", bufs=4))
@@ -118,39 +120,42 @@ def tile_hopfieldmemorylayer_pa_s_kernel(tc, query_input, norm_query_w, W_in, ou
             bias=mean_b_eps[:],
         )
 
-        h_rows = keep.tile([P, E], BF16)
+        h_rows = keep.tile([P, WORDS, 2 * P], BF16)
         g_bf16 = g_all[:].rearrange("r p i -> r (p i)").bitcast(BF16)
 
-        def normalise(s):
+        def normalise(j):
+            s, u = divmod(j, 2)
             cols = slice(s * K_PASS, (s + 1) * K_PASS)
             nc.vector.scalar_tensor_tensor(
-                out=h_rows[:, cols],
-                in0=x_sb[:, cols],
+                out=h_rows[:, j, :].rearrange("r (p e) -> r p e", e=2),
+                in0=x_sb[:, cols].rearrange("r (p u e) -> r u p e", u=2, e=2)[:, u, :, :],
                 scalar=inv_rms[:],
-                in1=g_bf16[:, cols],
+                in1=g_bf16[:, cols].rearrange("r (p u e) -> r u p e", u=2, e=2)[:, u, :, :],
                 op0=ALU.mult,
                 op1=ALU.mult,
             )
 
-        for s in range(PASSES):
-            normalise(s)
-
         w_codes = keep.tile([P, CHUNKS, PASSES * P], U32, align_bytes=64)
         w_scales = keep.tile([P, CHUNKS, PASSES * P], U8, align_bytes=64)
+        w_sorted = {}
         w_turned = {}
         w_grouped = {}
+
+        def sort_chunk(c):
+            w_sorted[c] = sorted_pool.tile([P, WORDS, P], F32, name="in_order", tag="in_order")
+            nc.vector.tensor_copy(
+                out=w_sorted[c][:].rearrange("o (s u) p -> o s u p", u=2),
+                in_=w_rows[c][:].bitcast(F32).rearrange("o (s p u) -> o s u p", s=PASSES, u=2),
+            )
 
         def transpose_chunk(c, passes=range(PASSES)):
             w_t = psum_w.tile([P, WORDS, P], F32, name="w_t", tag="w_t")
             words = w_rows[c][:].bitcast(F32)
             for s in passes:
                 for j in (2 * s, 2 * s + 1):
-                    nc.tensor.transpose(w_t[:, j, :], words[:, word_cols(j)], identity[:])
+                    in_words = w_sorted[c][:, j, :] if c in w_sorted else words[:, word_cols(j)]
+                    nc.tensor.transpose(w_t[:, j, :], in_words, identity[:])
                 w_turned[c, s] = w_t
-            if c < STREAM_WARM_UP:
-                nc.tensor.matmul(
-                    out=idle_bank[:], lhsT=identity[:], rhs=identity[:], start=True, stop=True
-                )
 
         def new_group(c):
             w_grouped[c] = grouped_pool.tile(
@@ -185,22 +190,16 @@ def tile_hopfieldmemorylayer_pa_s_kernel(tc, query_input, norm_query_w, W_in, ou
                 in_=w_grouped[c][:, s, :, :].rearrange("p o t -> p (o t)"),
             )
 
-        by_scalar = nc.scalar.copy
-        by_vector = nc.vector.tensor_copy
-
-        transpose_chunk(0)
-        regroup_chunk(0, by_scalar)
-        quantise_chunk(0)
-        transpose_chunk(1)
-        regroup_chunk(1, by_scalar)
-        quantise_chunk(1)
-        transpose_chunk(2)
-        regroup_chunk(2, by_scalar)
+        for j in range(WORDS):
+            normalise(j)
+        for c in range(FIRST_SORTED):
+            transpose_chunk(c)
+            regroup_chunk(c, nc.scalar.copy)
 
         h_t = psum_misc.tile([P, WORDS, P], F32, tag="bank")
         h_words = h_rows[:].bitcast(F32)
         for j in range(WORDS):
-            nc.tensor.transpose(h_t[:, j, :], h_words[:, word_cols(j)], identity[:])
+            nc.tensor.transpose(h_t[:, j, :], h_words[:, j, :], identity[:])
         h_grouped = keep.tile([P, PASSES, P, PACK], BF16, align_bytes=64)
         nc.scalar.copy(
             out=h_grouped[:].bitcast(F32), in_=h_t[:].rearrange("p (s u) r -> p s r u", u=2)
@@ -208,31 +207,29 @@ def tile_hopfieldmemorylayer_pa_s_kernel(tc, query_input, norm_query_w, W_in, ou
         h_codes = keep.tile([P, PASSES * P], U32, align_bytes=64)
         h_scales = keep.tile([P, PASSES * P], U8, align_bytes=64)
 
-        quantise_chunk(2)
-        transpose_chunk(3)
-        regroup_chunk(3, by_vector)
-        nc.vector.quantize_mx(
-            out=h_codes[:].bitcast(FP8X4),
-            scales=h_scales[:],
-            in_=h_grouped[:].rearrange("p s r t -> p (s r t)"),
-        )
-        transpose_chunk(4)
-        regroup_chunk(4, by_scalar)
-        quantise_chunk(3)
-        quantise_chunk(4)
-        transpose_chunk(5)
-        regroup_chunk(5, by_scalar)
-        quantise_chunk(5)
-        transpose_chunk(6)
-        regroup_chunk(6, by_scalar)
+        for c in range(FIRST_SORTED, CHUNKS):
+            sort_chunk(c)
+            if c == LAST:
+                for s in range(PASSES):
+                    transpose_chunk(c, (s,))
+                new_group(c)
+                for s in range(PASSES):
+                    regroup_pass(c, s, nc.scalar.copy)
+            else:
+                transpose_chunk(c)
+                regroup_chunk(c, nc.scalar.copy)
+            if c < 2 * FIRST_SORTED:
+                quantise_chunk(c - FIRST_SORTED)
+            elif c == 2 * FIRST_SORTED:
+                nc.vector.quantize_mx(
+                    out=h_codes[:].bitcast(FP8X4),
+                    scales=h_scales[:],
+                    in_=h_grouped[:].rearrange("p s r t -> p (s r t)"),
+                )
+        for c in range(FIRST_SORTED, LAST):
+            quantise_chunk(c)
         for s in range(PASSES):
-            transpose_chunk(7, (s,))
-        new_group(7)
-        regroup_pass(7, 0, by_vector)
-        regroup_pass(7, 1, by_scalar)
-        quantise_chunk(6)
-        quantise_pass(7, 0)
-        quantise_pass(7, 1)
+            quantise_pass(LAST, s)
 
         out_sb = keep.tile([P, E], F32)
         for pair in range(E // PAIR):
@@ -251,7 +248,7 @@ def tile_hopfieldmemorylayer_pa_s_kernel(tc, query_input, norm_query_w, W_in, ou
                         stop=(s == PASSES - 1),
                     )
             cols = slice(pair * PAIR, (pair + 1) * PAIR)
-            if pair == E // PAIR - 1:
+            if pair % 2 == 1:
                 nc.vector.tensor_copy(out=out_sb[:, cols], in_=acc[:])
             else:
                 nc.scalar.copy(out=out_sb[:, cols], in_=acc[:])

@@ -24,6 +24,7 @@ SCALAR_SQUARES = 640
 LAST = CHUNKS - 1
 FIRST_SORTED = 3
 HEAD_WARM_UP = 10
+STREAM_WARM_UP = 6
 
 FLOPS = 2 * P * E * E
 
@@ -156,6 +157,10 @@ def tile_hopfieldmemorylayer_pa_s_kernel(tc, query_input, norm_query_w, W_in, ou
                     in_words = w_sorted[c][:, j, :] if c in w_sorted else words[:, word_cols(j)]
                     nc.tensor.transpose(w_t[:, j, :], in_words, identity[:])
                 w_turned[c, s] = w_t
+            if c < STREAM_WARM_UP:
+                nc.tensor.matmul(
+                    out=idle_bank[:], lhsT=identity[:], rhs=identity[:], start=True, stop=True
+                )
 
         def new_group(c):
             w_grouped[c] = grouped_pool.tile(

@@ -22,9 +22,9 @@ CHUNKS = E // P
 PAIR = 2 * P
 SCALAR_SQUARES = 640
 LAST = CHUNKS - 1
-FIRST_SORTED = 3
+SORTED = 3
 HEAD_WARM_UP = 10
-STREAM_WARM_UP = 6
+STREAM_WARM_UP = 2
 
 FLOPS = 2 * P * E * E
 
@@ -42,7 +42,7 @@ def tile_hopfieldmemorylayer_pa_s_kernel(tc, query_input, norm_query_w, W_in, ou
     with ExitStack() as ctx:
         keep = ctx.enter_context(tc.tile_pool(name="keep", bufs=1))
         w_pool = ctx.enter_context(tc.tile_pool(name="w_rows", bufs=CHUNKS))
-        sorted_pool = ctx.enter_context(tc.tile_pool(name="w_sorted", bufs=CHUNKS - FIRST_SORTED))
+        sorted_pool = ctx.enter_context(tc.tile_pool(name="w_sorted", bufs=SORTED))
         grouped_pool = ctx.enter_context(tc.tile_pool(name="grouped", bufs=CHUNKS))
         psum_w = ctx.enter_context(tc.psum_pool(name="psum_w", bufs=4))
         psum_misc = ctx.enter_context(tc.psum_pool(name="psum_misc", bufs=4))
@@ -157,7 +157,9 @@ def tile_hopfieldmemorylayer_pa_s_kernel(tc, query_input, norm_query_w, W_in, ou
                     in_words = w_sorted[c][:, j, :] if c in w_sorted else words[:, word_cols(j)]
                     nc.tensor.transpose(w_t[:, j, :], in_words, identity[:])
                 w_turned[c, s] = w_t
-            if c < STREAM_WARM_UP:
+
+        def keep_clock():
+            for i in range(STREAM_WARM_UP):
                 nc.tensor.matmul(
                     out=idle_bank[:], lhsT=identity[:], rhs=identity[:], start=True, stop=True
                 )
@@ -197,9 +199,16 @@ def tile_hopfieldmemorylayer_pa_s_kernel(tc, query_input, norm_query_w, W_in, ou
 
         for j in range(WORDS):
             normalise(j)
-        for c in range(FIRST_SORTED):
-            transpose_chunk(c)
-            regroup_chunk(c, nc.scalar.copy)
+        by_scalar = nc.scalar.copy
+        by_vector = nc.vector.tensor_copy
+
+        transpose_chunk(0)
+        regroup_chunk(0, by_scalar)
+        transpose_chunk(1)
+        regroup_chunk(1, by_scalar)
+        keep_clock()
+        transpose_chunk(2)
+        regroup_chunk(2, by_scalar)
 
         h_t = psum_misc.tile([P, WORDS, P], F32, tag="bank")
         h_words = h_rows[:].bitcast(F32)
@@ -212,29 +221,38 @@ def tile_hopfieldmemorylayer_pa_s_kernel(tc, query_input, norm_query_w, W_in, ou
         h_codes = keep.tile([P, PASSES * P], U32, align_bytes=64)
         h_scales = keep.tile([P, PASSES * P], U8, align_bytes=64)
 
-        for c in range(FIRST_SORTED, CHUNKS):
-            sort_chunk(c)
-            if c == LAST:
-                for s in range(PASSES):
-                    transpose_chunk(c, (s,))
-                new_group(c)
-                for s in range(PASSES):
-                    regroup_pass(c, s, nc.scalar.copy)
-            else:
-                transpose_chunk(c)
-                regroup_chunk(c, nc.scalar.copy)
-            if c < 2 * FIRST_SORTED:
-                quantise_chunk(c - FIRST_SORTED)
-            elif c == 2 * FIRST_SORTED:
-                nc.vector.quantize_mx(
-                    out=h_codes[:].bitcast(FP8X4),
-                    scales=h_scales[:],
-                    in_=h_grouped[:].rearrange("p s r t -> p (s r t)"),
-                )
-        for c in range(FIRST_SORTED, LAST):
-            quantise_chunk(c)
+        quantise_chunk(0)
+        transpose_chunk(3)
+        regroup_chunk(3, by_scalar)
+        keep_clock()
+        sort_chunk(4)
+        transpose_chunk(4)
+        regroup_chunk(4, by_scalar)
+        sort_chunk(5)
+        transpose_chunk(5)
+        regroup_chunk(5, by_scalar)
+        keep_clock()
+        quantise_chunk(1)
+        sort_chunk(6)
+        transpose_chunk(6)
+        regroup_chunk(6, by_scalar)
+        quantise_chunk(2)
+        nc.vector.quantize_mx(
+            out=h_codes[:].bitcast(FP8X4),
+            scales=h_scales[:],
+            in_=h_grouped[:].rearrange("p s r t -> p (s r t)"),
+        )
+        quantise_chunk(3)
+        quantise_chunk(4)
         for s in range(PASSES):
-            quantise_pass(LAST, s)
+            transpose_chunk(LAST, (s,))
+        new_group(LAST)
+        regroup_pass(LAST, 0, by_vector)
+        regroup_pass(LAST, 1, by_scalar)
+        quantise_chunk(5)
+        quantise_pass(LAST, 0)
+        quantise_chunk(6)
+        quantise_pass(LAST, 1)
 
         out_sb = keep.tile([P, E], F32)
         for pair in range(E // PAIR):

@@ -49,7 +49,7 @@ def tile_hopfieldmemorylayer_pa_s_kernel(tc, query_input, norm_query_w, W_in, ou
         ctx.enter_context(tc.manual_schedule())
 
         g_sb = keep.tile([P, E // P], BF16)
-        nc.scalar.dma_start(out=g_sb[:], in_=norm_query_w.rearrange("(p c) -> p c", p=P))
+        nc.sync.dma_start(out=g_sb[:], in_=norm_query_w.rearrange("(p c) -> p c", p=P))
         x_sb = keep.tile([P, E], BF16)
         nc.sync.dma_start(out=x_sb[:], in_=x_dram)
         w_rows = []

@@ -19,10 +19,8 @@ K_PASS = P * PACK
 PASSES = E // K_PASS
 WORDS = 2 * PASSES
 CHUNKS = E // P
-PAIR = 2 * P
 SCALAR_SQUARES = 640
 LAST = CHUNKS - 1
-SORTED = 3
 HEAD_WARM_UP = 10
 STREAM_WARM_UP = 2
 
@@ -42,7 +40,6 @@ def tile_hopfieldmemorylayer_pa_s_kernel(tc, query_input, norm_query_w, W_in, ou
     with ExitStack() as ctx:
         keep = ctx.enter_context(tc.tile_pool(name="keep", bufs=1))
         w_pool = ctx.enter_context(tc.tile_pool(name="w_rows", bufs=CHUNKS))
-        sorted_pool = ctx.enter_context(tc.tile_pool(name="w_sorted", bufs=SORTED))
         grouped_pool = ctx.enter_context(tc.tile_pool(name="grouped", bufs=CHUNKS))
         psum_w = ctx.enter_context(tc.psum_pool(name="psum_w", bufs=4))
         psum_misc = ctx.enter_context(tc.psum_pool(name="psum_misc", bufs=4))
@@ -55,7 +52,10 @@ def tile_hopfieldmemorylayer_pa_s_kernel(tc, query_input, norm_query_w, W_in, ou
         w_rows = []
         for c in range(CHUNKS):
             rows = w_pool.tile([P, E], BF16, name="rows", tag="rows")
-            nc.sync.dma_start(out=rows[:], in_=W_in[c * P : (c + 1) * P, :])
+            pieces = PASSES if c == LAST else 1
+            for i in range(pieces):
+                cols = slice(i * E // pieces, (i + 1) * E // pieces)
+                nc.sync.dma_start(out=rows[:, cols], in_=W_in[c * P : (c + 1) * P, cols])
             w_rows.append(rows)
 
         identity = keep.tile([P, P], F32)
@@ -138,24 +138,15 @@ def tile_hopfieldmemorylayer_pa_s_kernel(tc, query_input, norm_query_w, W_in, ou
 
         w_codes = keep.tile([P, CHUNKS, PASSES * P], U32, align_bytes=64)
         w_scales = keep.tile([P, CHUNKS, PASSES * P], U8, align_bytes=64)
-        w_sorted = {}
         w_turned = {}
         w_grouped = {}
-
-        def sort_chunk(c):
-            w_sorted[c] = sorted_pool.tile([P, WORDS, P], F32, name="in_order", tag="in_order")
-            nc.vector.tensor_copy(
-                out=w_sorted[c][:].rearrange("o (s u) p -> o s u p", u=2),
-                in_=w_rows[c][:].bitcast(F32).rearrange("o (s p u) -> o s u p", s=PASSES, u=2),
-            )
 
         def transpose_chunk(c, passes=range(PASSES)):
             w_t = psum_w.tile([P, WORDS, P], F32, name="w_t", tag="w_t")
             words = w_rows[c][:].bitcast(F32)
             for s in passes:
                 for j in (2 * s, 2 * s + 1):
-                    in_words = w_sorted[c][:, j, :] if c in w_sorted else words[:, word_cols(j)]
-                    nc.tensor.transpose(w_t[:, j, :], in_words, identity[:])
+                    nc.tensor.transpose(w_t[:, j, :], words[:, word_cols(j)], identity[:])
                 w_turned[c, s] = w_t
 
         def keep_clock():
@@ -209,6 +200,10 @@ def tile_hopfieldmemorylayer_pa_s_kernel(tc, query_input, norm_query_w, W_in, ou
         keep_clock()
         transpose_chunk(2)
         regroup_chunk(2, by_scalar)
+        quantise_chunk(0)
+        quantise_chunk(1)
+        transpose_chunk(3)
+        regroup_chunk(3, by_vector)
 
         h_t = psum_misc.tile([P, WORDS, P], F32, tag="bank")
         h_words = h_rows[:].bitcast(F32)
@@ -221,29 +216,21 @@ def tile_hopfieldmemorylayer_pa_s_kernel(tc, query_input, norm_query_w, W_in, ou
         h_codes = keep.tile([P, PASSES * P], U32, align_bytes=64)
         h_scales = keep.tile([P, PASSES * P], U8, align_bytes=64)
 
-        quantise_chunk(0)
-        transpose_chunk(3)
-        regroup_chunk(3, by_scalar)
-        keep_clock()
-        sort_chunk(4)
+        quantise_chunk(2)
         transpose_chunk(4)
         regroup_chunk(4, by_scalar)
-        sort_chunk(5)
-        transpose_chunk(5)
-        regroup_chunk(5, by_scalar)
         keep_clock()
-        quantise_chunk(1)
-        sort_chunk(6)
-        transpose_chunk(6)
-        regroup_chunk(6, by_scalar)
-        quantise_chunk(2)
         nc.vector.quantize_mx(
             out=h_codes[:].bitcast(FP8X4),
             scales=h_scales[:],
             in_=h_grouped[:].rearrange("p s r t -> p (s r t)"),
         )
         quantise_chunk(3)
+        transpose_chunk(5)
+        regroup_chunk(5, by_scalar)
         quantise_chunk(4)
+        transpose_chunk(6)
+        regroup_chunk(6, by_scalar)
         for s in range(PASSES):
             transpose_chunk(LAST, (s,))
         new_group(LAST)
@@ -255,24 +242,30 @@ def tile_hopfieldmemorylayer_pa_s_kernel(tc, query_input, norm_query_w, W_in, ou
         quantise_pass(LAST, 1)
 
         out_sb = keep.tile([P, E], F32)
-        for pair in range(E // PAIR):
-            acc = psum_misc.tile([P, PAIR], F32, tag="bank")
-            for half in range(2):
-                c = 2 * pair + half
-                for s in range(PASSES):
-                    k_cols = slice(s * P, (s + 1) * P)
-                    nc.tensor.matmul_mx(
-                        out=acc[:, half * P : (half + 1) * P],
-                        lhsT=h_codes[:, k_cols].bitcast(FP8X4),
-                        lhsT_scale=h_scales[:, k_cols],
-                        rhs=w_codes[:, c, k_cols].bitcast(FP8X4),
-                        rhs_scale=w_scales[:, c, k_cols],
-                        start=(s == 0),
-                        stop=(s == PASSES - 1),
-                    )
-            cols = slice(pair * PAIR, (pair + 1) * PAIR)
-            if pair % 2 == 1:
-                nc.vector.tensor_copy(out=out_sb[:, cols], in_=acc[:])
-            else:
-                nc.scalar.copy(out=out_sb[:, cols], in_=acc[:])
+
+        def multiply(c, acc):
+            for s in range(PASSES):
+                k_cols = slice(s * P, (s + 1) * P)
+                nc.tensor.matmul_mx(
+                    out=acc,
+                    lhsT=h_codes[:, k_cols].bitcast(FP8X4),
+                    lhsT_scale=h_scales[:, k_cols],
+                    rhs=w_codes[:, c, k_cols].bitcast(FP8X4),
+                    rhs_scale=w_scales[:, c, k_cols],
+                    start=(s == 0),
+                    stop=(s == PASSES - 1),
+                )
+
+        for group, copy in (
+            ((0, 1), by_vector),
+            ((2, 3), by_vector),
+            ((4, 5), by_scalar),
+            ((6,), by_vector),
+            ((7,), by_scalar),
+        ):
+            cols = slice(group[0] * P, (group[-1] + 1) * P)
+            acc = psum_misc.tile([P, len(group) * P], F32, tag="bank")
+            for i, c in enumerate(group):
+                multiply(c, acc[:, i * P : (i + 1) * P])
+            copy(out=out_sb[:, cols], in_=acc[:])
             nc.sync.dma_start(out=out_dram[:, cols], in_=out_sb[:, cols])

@@ -22,7 +22,7 @@ CHUNKS = E // P
 SCALAR_SQUARES = 640
 LAST = CHUNKS - 1
 HEAD_WARM_UP = 10
-STREAM_WARM_UP = 2
+STREAM_WARM_UP = 6
 
 FLOPS = 2 * P * E * E
 
@@ -45,8 +45,10 @@ def tile_hopfieldmemorylayer_pa_s_kernel(tc, query_input, norm_query_w, W_in, ou
         psum_misc = ctx.enter_context(tc.psum_pool(name="psum_misc", bufs=4))
         ctx.enter_context(tc.manual_schedule())
 
-        g_sb = keep.tile([P, E // P], BF16)
-        nc.sync.dma_start(out=g_sb[:], in_=norm_query_w.rearrange("(p c) -> p c", p=P))
+        g_sb = keep.tile([P, PASSES, PACK], BF16)
+        nc.scalar.dma_start(
+            out=g_sb[:], in_=norm_query_w.rearrange("(s p t) -> p s t", s=PASSES, t=PACK)
+        )
         x_sb = keep.tile([P, E], BF16)
         nc.sync.dma_start(out=x_sb[:], in_=x_dram)
         w_rows = []
@@ -85,12 +87,10 @@ def tile_hopfieldmemorylayer_pa_s_kernel(tc, query_input, norm_query_w, W_in, ou
                 stop=True,
             )
 
-        g_all = psum_misc.tile([P, P, WORDS], F32, tag="bank")
-        g_words = g_sb[:].bitcast(F32)
-        for i in range(WORDS):
-            nc.tensor.transpose(
-                g_all[:, :, i], g_words[:, i : i + 1].to_broadcast([P, P]), identity[:]
-            )
+        x_t = psum_misc.tile([P, WORDS, P], F32, tag="bank")
+        x_words = x_sb[:].bitcast(F32)
+        for j in range(WORDS):
+            nc.tensor.transpose(x_t[:, j, :], x_words[:, word_cols(j)], identity[:])
 
         squares_a = keep.tile([P, SCALAR_SQUARES], F32)
         sum_a = keep.tile([P, 1], F32)
@@ -121,19 +121,18 @@ def tile_hopfieldmemorylayer_pa_s_kernel(tc, query_input, norm_query_w, W_in, ou
             bias=mean_b_eps[:],
         )
 
-        h_rows = keep.tile([P, WORDS, 2 * P], BF16)
-        g_bf16 = g_all[:].rearrange("r p i -> r (p i)").bitcast(BF16)
-
-        def normalise(j):
-            s, u = divmod(j, 2)
-            cols = slice(s * K_PASS, (s + 1) * K_PASS)
-            nc.vector.scalar_tensor_tensor(
-                out=h_rows[:, j, :].rearrange("r (p e) -> r p e", e=2),
-                in0=x_sb[:, cols].rearrange("r (p u e) -> r u p e", u=2, e=2)[:, u, :, :],
-                scalar=inv_rms[:],
-                in1=g_bf16[:, cols].rearrange("r (p u e) -> r u p e", u=2, e=2)[:, u, :, :],
-                op0=ALU.mult,
-                op1=ALU.mult,
+        xg = keep.tile([P, PASSES, P, PACK], F32)
+        for s in range(PASSES):
+            nc.vector.tensor_tensor(
+                out=xg[:, s, :, :].rearrange("p r (u e) -> p r u e", e=2),
+                in0=x_t[:, 2 * s : 2 * s + 2, :]
+                .bitcast(BF16)
+                .rearrange("p u (r e) -> p r u e", e=2),
+                in1=g_sb[:, s, :]
+                .rearrange("p (u e) -> p u e", e=2)
+                .unsqueeze(1)
+                .to_broadcast([P, P, 2, 2]),
+                op=ALU.mult,
             )
 
         w_codes = keep.tile([P, CHUNKS, PASSES * P], U32, align_bytes=64)
@@ -148,9 +147,7 @@ def tile_hopfieldmemorylayer_pa_s_kernel(tc, query_input, norm_query_w, W_in, ou
                 for j in (2 * s, 2 * s + 1):
                     nc.tensor.transpose(w_t[:, j, :], words[:, word_cols(j)], identity[:])
                 w_turned[c, s] = w_t
-
-        def keep_clock():
-            for i in range(STREAM_WARM_UP):
+            if c < STREAM_WARM_UP:
                 nc.tensor.matmul(
                     out=idle_bank[:], lhsT=identity[:], rhs=identity[:], start=True, stop=True
                 )
@@ -188,57 +185,43 @@ def tile_hopfieldmemorylayer_pa_s_kernel(tc, query_input, norm_query_w, W_in, ou
                 in_=w_grouped[c][:, s, :, :].rearrange("p o t -> p (o t)"),
             )
 
-        for j in range(WORDS):
-            normalise(j)
         by_scalar = nc.scalar.copy
         by_vector = nc.vector.tensor_copy
 
-        transpose_chunk(0)
-        regroup_chunk(0, by_scalar)
-        transpose_chunk(1)
-        regroup_chunk(1, by_scalar)
-        keep_clock()
-        transpose_chunk(2)
-        regroup_chunk(2, by_scalar)
-        quantise_chunk(0)
-        quantise_chunk(1)
-        transpose_chunk(3)
-        regroup_chunk(3, by_vector)
+        for c in range(2):
+            transpose_chunk(c)
+            regroup_chunk(c, by_scalar)
 
-        h_t = psum_misc.tile([P, WORDS, P], F32, tag="bank")
-        h_words = h_rows[:].bitcast(F32)
-        for j in range(WORDS):
-            nc.tensor.transpose(h_t[:, j, :], h_words[:, j, :], identity[:])
+        inv_rms_t = psum_misc.tile([P, P], F32, tag="bank")
+        nc.tensor.transpose(inv_rms_t[:], inv_rms[:, 0:1].to_broadcast([P, P]), identity[:])
         h_grouped = keep.tile([P, PASSES, P, PACK], BF16, align_bytes=64)
-        nc.scalar.copy(
-            out=h_grouped[:].bitcast(F32), in_=h_t[:].rearrange("p (s u) r -> p s r u", u=2)
-        )
+        for s in range(PASSES):
+            nc.vector.tensor_tensor(
+                out=h_grouped[:, s, :, :],
+                in0=xg[:, s, :, :],
+                in1=inv_rms_t[:].unsqueeze(2).to_broadcast([P, P, PACK]),
+                op=ALU.mult,
+            )
         h_codes = keep.tile([P, PASSES * P], U32, align_bytes=64)
         h_scales = keep.tile([P, PASSES * P], U8, align_bytes=64)
-
-        quantise_chunk(2)
-        transpose_chunk(4)
-        regroup_chunk(4, by_scalar)
-        keep_clock()
         nc.vector.quantize_mx(
             out=h_codes[:].bitcast(FP8X4),
             scales=h_scales[:],
             in_=h_grouped[:].rearrange("p s r t -> p (s r t)"),
         )
-        quantise_chunk(3)
-        transpose_chunk(5)
-        regroup_chunk(5, by_scalar)
-        quantise_chunk(4)
-        transpose_chunk(6)
-        regroup_chunk(6, by_scalar)
+
+        for c in range(2, LAST):
+            transpose_chunk(c)
+            regroup_chunk(c, by_scalar)
+            quantise_chunk(c - 2)
         for s in range(PASSES):
             transpose_chunk(LAST, (s,))
         new_group(LAST)
         regroup_pass(LAST, 0, by_vector)
         regroup_pass(LAST, 1, by_scalar)
-        quantise_chunk(5)
+        quantise_chunk(LAST - 2)
         quantise_pass(LAST, 0)
-        quantise_chunk(6)
+        quantise_chunk(LAST - 1)
         quantise_pass(LAST, 1)
 
         out_sb = keep.tile([P, E], F32)
@@ -257,15 +240,21 @@ def tile_hopfieldmemorylayer_pa_s_kernel(tc, query_input, norm_query_w, W_in, ou
                 )
 
         for group, copy in (
-            ((0, 1), by_vector),
-            ((2, 3), by_vector),
+            ((0, 1), by_scalar),
+            ((2, 3), by_scalar),
             ((4, 5), by_scalar),
             ((6,), by_vector),
             ((7,), by_scalar),
         ):
             cols = slice(group[0] * P, (group[-1] + 1) * P)
-            acc = psum_misc.tile([P, len(group) * P], F32, tag="bank")
+            if len(group) == 1:
+                acc = psum_w.tile([P, WORDS, P], F32, name="w_t", tag="w_t")
+            else:
+                acc = psum_misc.tile([P, WORDS, P], F32, tag="bank")
             for i, c in enumerate(group):
-                multiply(c, acc[:, i * P : (i + 1) * P])
-            copy(out=out_sb[:, cols], in_=acc[:])
+                multiply(c, acc[:, i, :])
+            copy(
+                out=out_sb[:, cols].rearrange("r (i o) -> r i o", o=P),
+                in_=acc[:, 0 : len(group), :],
+            )
             nc.sync.dma_start(out=out_dram[:, cols], in_=out_sb[:, cols])

from contextlib import ExitStack

import concourse.mybir as mybir
from concourse.masks import make_identity

F32 = mybir.dt.float32
BF16 = mybir.dt.bfloat16
U32 = mybir.dt.uint32
U8 = mybir.dt.uint8
FP8X4 = mybir.dt.float8_e4m3fn_x4
ACT = mybir.ActivationFunctionType
ALU = mybir.AluOpType

P = 128
E = 1024
EPS = 1e-6
PACK = 4
K_PASS = P * PACK
PASSES = E // K_PASS
WORDS = 2 * PASSES
CHUNKS = E // P
SCALAR_SQUARES = 640
LAST = CHUNKS - 1
HEAD_WARM_UP = 10
STREAM_WARM_UP = 6

FLOPS = 2 * P * E * E


def word_cols(j):
    s, u = divmod(j, 2)
    return slice(2 * P * s + u, 2 * P * (s + 1), 2)


def tile_hopfieldmemorylayer_pa_s_kernel(tc, query_input, norm_query_w, W_in, out):
    nc = tc.nc
    x_dram = query_input.flatten_outer_dims()
    out_dram = out.flatten_outer_dims()

    with ExitStack() as ctx:
        keep = ctx.enter_context(tc.tile_pool(name="keep", bufs=1))
        w_pool = ctx.enter_context(tc.tile_pool(name="w_rows", bufs=CHUNKS))
        grouped_pool = ctx.enter_context(tc.tile_pool(name="grouped", bufs=CHUNKS))
        psum_w = ctx.enter_context(tc.psum_pool(name="psum_w", bufs=4))
        psum_misc = ctx.enter_context(tc.psum_pool(name="psum_misc", bufs=4))
        ctx.enter_context(tc.manual_schedule())

        g_sb = keep.tile([P, PASSES, PACK], BF16)
        nc.scalar.dma_start(
            out=g_sb[:], in_=norm_query_w.rearrange("(s p t) -> p s t", s=PASSES, t=PACK)
        )
        x_sb = keep.tile([P, E], BF16)
        nc.sync.dma_start(out=x_sb[:], in_=x_dram)
        w_rows = []
        for c in range(CHUNKS):
            rows = w_pool.tile([P, E], BF16, name="rows", tag="rows")
            pieces = PASSES if c == LAST else 1
            for i in range(pieces):
                cols = slice(i * E // pieces, (i + 1) * E // pieces)
                nc.sync.dma_start(out=rows[:, cols], in_=W_in[c * P : (c + 1) * P, cols])
            w_rows.append(rows)

        identity = keep.tile([P, P], F32)
        make_identity(nc, identity[:])

        one = keep.tile([P, 1], F32)
        nc.gpsimd.memset(one[:], 1.0)
        table_warmer = keep.tile([P, 1], F32)
        nc.scalar.activation(out=table_warmer[:], in_=one[:], func=ACT.Abs_reciprocal_sqrt)

        idle_values = keep.tile([P, K_PASS], BF16, align_bytes=64)
        nc.vector.memset(idle_values[:].bitcast(F32), 0.0)
        idle_codes = keep.tile([P, P], U32, align_bytes=64)
        idle_scales = keep.tile([P, P], U8, align_bytes=64)
        nc.vector.quantize_mx(
            out=idle_codes[:].bitcast(FP8X4), scales=idle_scales[:], in_=idle_values[:]
        )
        idle_bank = psum_misc.tile([P, P], F32, tag="bank")
        for i in range(HEAD_WARM_UP):
            nc.tensor.matmul_mx(
                out=idle_bank[:],
                lhsT=idle_codes[:].bitcast(FP8X4),
                lhsT_scale=idle_scales[:],
                rhs=idle_codes[:].bitcast(FP8X4),
                rhs_scale=idle_scales[:],
                start=True,
                stop=True,
            )

        x_t = psum_misc.tile([P, WORDS, P], F32, tag="bank")
        x_words = x_sb[:].bitcast(F32)
        for j in range(WORDS):
            nc.tensor.transpose(x_t[:, j, :], x_words[:, word_cols(j)], identity[:])

        squares_a = keep.tile([P, SCALAR_SQUARES], F32)
        sum_a = keep.tile([P, 1], F32)
        nc.scalar.activation(
            out=squares_a[:], in_=x_sb[:, 0:SCALAR_SQUARES], func=ACT.Square, accum_out=sum_a[:]
        )
        squares_b = keep.tile([P, E - SCALAR_SQUARES], F32)
        sum_b = keep.tile([P, 1], F32)
        nc.vector.scalar_tensor_tensor(
            out=squares_b[:],
            in0=x_sb[:, SCALAR_SQUARES:E],
            scalar=1.0,
            in1=x_sb[:, SCALAR_SQUARES:E],
            op0=ALU.mult,
            op1=ALU.mult,
            accum_out=sum_b[:],
        )
        mean_b_eps = keep.tile([P, 1], F32)
        nc.vector.tensor_scalar(
            out=mean_b_eps[:], in0=sum_b[:], scalar1=1.0 / E, scalar2=EPS, op0=ALU.mult, op1=ALU.add
        )
        inv_rms = keep.tile([P, 1], F32)
        nc.scalar.activation(
            out=inv_rms[:],
            in_=sum_a[:],
            func=ACT.Abs_reciprocal_sqrt,
            scale=1.0 / E,
            bias=mean_b_eps[:],
        )

        xg = keep.tile([P, PASSES, P, PACK], F32)
        for s in range(PASSES):
            nc.vector.tensor_tensor(
                out=xg[:, s, :, :].rearrange("p r (u e) -> p r u e", e=2),
                in0=x_t[:, 2 * s : 2 * s + 2, :]
                .bitcast(BF16)
                .rearrange("p u (r e) -> p r u e", e=2),
                in1=g_sb[:, s, :]
                .rearrange("p (u e) -> p u e", e=2)
                .unsqueeze(1)
                .to_broadcast([P, P, 2, 2]),
                op=ALU.mult,
            )

        w_codes = keep.tile([P, CHUNKS, PASSES * P], U32, align_bytes=64)
        w_scales = keep.tile([P, CHUNKS, PASSES * P], U8, align_bytes=64)
        w_turned = {}
        w_grouped = {}

        def transpose_chunk(c, passes=range(PASSES)):
            w_t = psum_w.tile([P, WORDS, P], F32, name="w_t", tag="w_t")
            words = w_rows[c][:].bitcast(F32)
            for s in passes:
                for j in (2 * s, 2 * s + 1):
                    nc.tensor.transpose(w_t[:, j, :], words[:, word_cols(j)], identity[:])
                w_turned[c, s] = w_t
            if c < STREAM_WARM_UP:
                nc.tensor.matmul(
                    out=idle_bank[:], lhsT=identity[:], rhs=identity[:], start=True, stop=True
                )

        def new_group(c):
            w_grouped[c] = grouped_pool.tile(
                [P, PASSES, P, PACK], BF16, name="grouped", tag="grouped", align_bytes=64
            )

        def regroup_chunk(c, copy):
            new_group(c)
            copy(
                out=w_grouped[c][:].bitcast(F32),
                in_=w_turned[c, 0][:].rearrange("p (s u) o -> p s o u", u=2),
            )

        def regroup_pass(c, s, copy):
            copy(
                out=w_grouped[c][:, s, :, :].bitcast(F32),
                in_=w_turned[c, s][:, 2 * s : 2 * s + 2, :].rearrange("p u o -> p o u"),
            )

        def quantise_chunk(c):
            nc.vector.quantize_mx(
                out=w_codes[:, c, :].bitcast(FP8X4),
                scales=w_scales[:, c, :],
                in_=w_grouped[c][:].rearrange("p s o t -> p (s o t)"),
            )

        def quantise_pass(c, s):
            cols = slice(s * P, (s + 1) * P)
            nc.vector.quantize_mx(
                out=w_codes[:, c, cols].bitcast(FP8X4),
                scales=w_scales[:, c, cols],
                in_=w_grouped[c][:, s, :, :].rearrange("p o t -> p (o t)"),
            )

        by_scalar = nc.scalar.copy
        by_vector = nc.vector.tensor_copy

        for c in range(2):
            transpose_chunk(c)
            regroup_chunk(c, by_scalar)

        inv_rms_t = psum_misc.tile([P, P], F32, tag="bank")
        nc.tensor.transpose(inv_rms_t[:], inv_rms[:, 0:1].to_broadcast([P, P]), identity[:])
        h_grouped = keep.tile([P, PASSES, P, PACK], BF16, align_bytes=64)
        for s in range(PASSES):
            nc.vector.tensor_tensor(
                out=h_grouped[:, s, :, :],
                in0=xg[:, s, :, :],
                in1=inv_rms_t[:].unsqueeze(2).to_broadcast([P, P, PACK]),
                op=ALU.mult,
            )
        h_codes = keep.tile([P, PASSES * P], U32, align_bytes=64)
        h_scales = keep.tile([P, PASSES * P], U8, align_bytes=64)
        nc.vector.quantize_mx(
            out=h_codes[:].bitcast(FP8X4),
            scales=h_scales[:],
            in_=h_grouped[:].rearrange("p s r t -> p (s r t)"),
        )

        for c in range(2, LAST):
            transpose_chunk(c)
            regroup_chunk(c, by_scalar)
            quantise_chunk(c - 2)
        for s in range(PASSES):
            transpose_chunk(LAST, (s,))
        new_group(LAST)
        regroup_pass(LAST, 0, by_vector)
        regroup_pass(LAST, 1, by_scalar)
        quantise_chunk(LAST - 2)
        quantise_pass(LAST, 0)
        quantise_chunk(LAST - 1)
        quantise_pass(LAST, 1)

        out_sb = keep.tile([P, E], F32)

        def multiply(c, acc):
            for s in range(PASSES):
                k_cols = slice(s * P, (s + 1) * P)
                nc.tensor.matmul_mx(
                    out=acc,
                    lhsT=h_codes[:, k_cols].bitcast(FP8X4),
                    lhsT_scale=h_scales[:, k_cols],
                    rhs=w_codes[:, c, k_cols].bitcast(FP8X4),
                    rhs_scale=w_scales[:, c, k_cols],
                    start=(s == 0),
                    stop=(s == PASSES - 1),
                )

        for group, copy in (
            ((0, 1), by_scalar),
            ((2, 3), by_scalar),
            ((4, 5), by_scalar),
            ((6,), by_vector),
            ((7,), by_scalar),
        ):
            cols = slice(group[0] * P, (group[-1] + 1) * P)
            if len(group) == 1:
                acc = psum_w.tile([P, WORDS, P], F32, name="w_t", tag="w_t")
            else:
                acc = psum_misc.tile([P, WORDS, P], F32, tag="bank")
            for i, c in enumerate(group):
                multiply(c, acc[:, i, :])
            copy(
                out=out_sb[:, cols].rearrange("r (i o) -> r i o", o=P),
                in_=acc[:, 0 : len(group), :],
            )
            nc.sync.dma_start(out=out_dram[:, cols], in_=out_sb[:, cols])
